import numpy as np
import ml_dtypes


def mxq(x, axis, fmt="e4m3"):
    dtype, down = {"e4m3": (ml_dtypes.float8_e4m3fn, 7), "e5m2": (ml_dtypes.float8_e5m2, 14)}[fmt]
    v = np.moveaxis(np.asarray(x, np.float32).astype(ml_dtypes.bfloat16).astype(np.float64), axis, -1)
    blocks = v.reshape(v.shape[:-1] + (-1, 32))
    amax = np.abs(blocks).max(-1, keepdims=True)
    byte = np.maximum(np.where(amax > 0, np.frexp(amax)[1] - 1 + 127, 0) - down, 1)
    scale = np.exp2(byte - 127.0)
    codes = (blocks / scale).astype(np.float32).astype(dtype).astype(np.float64)
    return np.moveaxis((codes * scale).reshape(v.shape), -1, axis)


WIDE = False


def mx_kscale(k):
    if not WIDE:
        return np.ones(k)
    levels = np.array([10, -10, 5, -5, 0])
    a = np.random.permutation(np.resize(levels, k // 512 * 4)).reshape(k // 512, 4)
    idx = np.arange(k)
    return np.exp2(a[idx // 512, idx % 128 // 32])


BF16 = ml_dtypes.bfloat16


def bf(x):
    return np.asarray(x, np.float32).astype(BF16)


def f64(x):
    return np.asarray(x).astype(np.float64)


B, C, O, H, W, KH, KW, PAD = 4, 512, 256, 32, 32, 3, 3, 1
C_CURV = 0.01
EPS = 1e-7


def artanh(z):
    return 0.5 * np.log((1.0 + z) / (1.0 - z))


def log0(y):
    sqc = np.sqrt(C_CURV)
    n = np.maximum(np.sqrt((y * y).sum(-1, keepdims=True)), EPS)
    return artanh(np.clip(sqc * n, 0.0, 1.0 - 1e-6)) * y / (sqc * n)


def exp0(v):
    sqc = np.sqrt(C_CURV)
    n = np.maximum(np.sqrt((v * v).sum(-1, keepdims=True)), EPS)
    return np.tanh(sqc * n) * v / (sqc * n)


def setup_inputs():
    s = mx_kscale(C)
    rho = np.sqrt(np.mean(s * s))
    raw = np.random.uniform(0.0, 1.0, (B, C, H, W)) * s[None, :, None, None]
    r = np.random.uniform(0.2, 0.85, (B, 1, H, W))
    x = raw / np.sqrt((raw * raw).sum(1, keepdims=True)) * r / np.sqrt(C_CURV)
    return {"x": bf(x),
            "Wk": bf(np.random.standard_normal((KH * KW, O, C)) * 2.1 / np.sqrt(KH * KW * O) * rho / s),
            "bias": bf(np.random.standard_normal(O) * 5.0 / np.sqrt(O))}


def reference(x, Wk, bias):
    Hout, Wout = H + 2 * PAD - KH + 1, W + 2 * PAD - KW + 1
    u = log0(np.moveaxis(f64(x), 1, -1)).reshape(B * H * W, C)
    w = f64(Wk).transpose(2, 0, 1).reshape(C, KH * KW * O)
    y = mxq(u, 1, "e4m3") @ mxq(w, 0, "e4m3")
    yp = np.pad(y.reshape(B, H, W, KH * KW, O), ((0, 0), (PAD, PAD), (PAD, PAD), (0, 0), (0, 0)))
    v = sum(yp[:, i:i + Hout, j:j + Wout, KW * i + j, :] for i in range(KH) for j in range(KW))
    v = np.maximum(v + f64(bias), 0.0)
    out = exp0(v)
    return np.transpose(out, (0, 3, 1, 2))

@@ -1,0 +1,349 @@
+from contextlib import ExitStack
+
+import concourse.mybir as mybir
+from concourse.masks import make_identity
+
+FP8X4 = mybir.dt.float8_e4m3fn_x4
+BF16 = mybir.dt.bfloat16
+F32 = mybir.dt.float32
+I32 = mybir.dt.int32
+U32 = mybir.dt.uint32
+U8 = mybir.dt.uint8
+ALU = mybir.AluOpType
+ACT = mybir.ActivationFunctionType
+
+P = 128
+B, C, O, H, W = 4, 512, 256, 32, 32
+FLOPS = 2 * B * H * W * C * 9 * O
+ZMAX = 1.0 - 1e-6
+ROWS = 8
+NCH = 8
+PADW = (H + 2) * 64
+ACC_BUFS, TP_BUFS, BC_BUFS = 3, 2, 3
+EARLY_RELU = 2
+EARLY_COPY = 4
+
+
+def tile_pvconv2d_t_kernel(tc, x, Wk, bias, out):
+    nc = tc.nc
+    with ExitStack() as ctx:
+        ctx.enter_context(tc.manual_schedule())
+        const = ctx.enter_context(tc.tile_pool(name="const", bufs=1))
+        upool = ctx.enter_context(tc.tile_pool(name="upool", bufs=2))
+        junkp = ctx.enter_context(tc.tile_pool(name="junkp", bufs=2))
+        rpool = ctx.enter_context(tc.tile_pool(name="rpool", bufs=10))
+        opool = ctx.enter_context(tc.tile_pool(name="opool", bufs=4))
+        tp = ctx.enter_context(tc.psum_pool(name="tp", bufs=TP_BUFS))
+        bc = ctx.enter_context(tc.psum_pool(name="bc", bufs=BC_BUFS))
+        accp = ctx.enter_context(tc.psum_pool(name="accp", bufs=ACC_BUFS))
+
+        ident_f = const.tile([P, P], F32, name="ident_f")
+        make_identity(nc, ident_f[:])
+        ident_b = const.tile([P, P], BF16, name="ident_b")
+        make_identity(nc, ident_b[:])
+        ones1 = const.tile([P, 1], F32, name="ones1")
+        nc.vector.memset(ones1[:], 1.0)
+        mhalf4 = const.tile([P, 4], F32, name="mhalf4")
+        nc.vector.memset(mhalf4[:], -0.5)
+        zeros = const.tile([P, 16, 4], BF16, name="zeros")
+        nc.vector.memset(zeros[:], 0.0)
+        warm = const.tile([P, 1], F32, name="warm")
+        nc.scalar.activation(out=warm[:], in_=ones1[:], func=ACT.Ln)
+        btile = const.tile([P, P], BF16, name="btile")
+        nc.vector.memset(btile[:], 0.0)
+
+        codes = [[const.tile([P, PADW], U32, name="codes%d%d" % (j, bp), align_bytes=64) for bp in range(2)] for j in range(3)]
+        planes = [[const.tile([P, PADW], U8, name="planes%d%d" % (j, bp), align_bytes=64) for bp in range(2)] for j in range(3)]
+        ul = [const.tile([P, 16, 128], BF16, name="ul%d" % k, align_bytes=64) for k in range(2)]
+        ur = [const.tile([P, 16, 128], BF16, name="ur%d" % k, align_bytes=64) for k in range(2)]
+        for k in range(2):
+            nc.vector.memset(ul[k][:, :, 0:4], 0.0)
+            nc.scalar.copy(out=ur[k][:, :, 124:128], in_=zeros[:])
+        for j in range(3):
+            for bp in range(2):
+                for lo in (0, PADW - 64):
+                    nc.vector.memset(codes[j][bp][:, lo:lo + 64].bitcast(I32), 0)
+                    nc.vector.memset(planes[j][bp][:, lo:lo + 64].bitcast(I32), 0)
+
+        names = ["n2", "y4", "z2", "zc", "la", "lb", "rzh", "dd", "gg", "m2", "y2o", "zm", "th", "rzo", "tf"]
+        sm = dict((nm, const.tile([P, 4 * NCH], F32, name="sm_" + nm)) for nm in names)
+
+        def s4(nm, c):
+            return sm[nm][:, 4 * c:4 * c + 4]
+
+        xs = [const.tile([P, 4, H * W], BF16, name="xs%d" % b) for b in range(B)]
+        w_sb = const.tile([P, 18, C], BF16, name="w_sb")
+        wk_v = Wk.rearrange("k (h p) c -> p (k h) c", p=P)
+
+        def load_x(b):
+            nc.sync.dma_start(
+                out=xs[b][:].rearrange("q (u e) n -> q u (e n)", u=2),
+                in_=x[b].rearrange("(u q e) h w -> q u (e h w)", u=2, q=P, e=2),
+            )
+
+        def load_x_half(b, hh):
+            xv = x[b].rearrange("(u q e) h w -> u q e (h w)", u=2, q=P, e=2)
+            for u in range(2):
+                nc.sync.dma_start(out=xs[b][:, 2 * u:2 * u + 2, hh * 512:(hh + 1) * 512],
+                                  in_=xv[u][:, :, hh * 512:(hh + 1) * 512])
+
+        def load_w(k3):
+            nc.sync.dma_start(out=w_sb[:, 6 * k3:6 * k3 + 6, :], in_=wk_v[:, 6 * k3:6 * k3 + 6, :])
+
+        nc.scalar.dma_start(out=btile[0:2, :], in_=bias.rearrange("(h o) -> h o", h=2))
+        load_x_half(0, 0)
+        load_x_half(1, 0)
+        load_w(0)
+        load_w(1)
+        load_w(2)
+        load_x_half(0, 1)
+        load_x_half(1, 1)
+        load_x_half(2, 0)
+        load_x_half(3, 0)
+        load_x_half(2, 1)
+        load_x_half(3, 1)
+
+        wg = const.tile([P, 18, P, 4], BF16, name="wg", align_bytes=64)
+        wc = const.tile([P, 18 * P], U32, name="wc", align_bytes=64)
+        ws = const.tile([P, 18 * P], U8, name="ws", align_bytes=64)
+        w_f = w_sb[:].bitcast(F32)
+        wg_f = wg[:].bitcast(F32)
+
+        def w_transpose(k):
+            wt = accp.tile([P, 2, 2, P], F32, name="wt", tag="acc")
+            for bl in range(2):
+                for u in range(2):
+                    nc.tensor.transpose(wt[:, bl, u, :], w_f[:, 2 * k + bl, u * P:(u + 1) * P], ident_f[:])
+            if k < 3:
+                nc.vector.tensor_copy(out=wg_f[:, 2 * k:2 * k + 2, :, :], in_=wt[:].rearrange("p b u o -> p b o u"))
+            else:
+                nc.scalar.copy(out=wg_f[:, 2 * k:2 * k + 2, :, :], in_=wt[:].rearrange("p b u o -> p b o u"))
+
+        def w_quant(k):
+            nc.vector.quantize_mx(
+                out=wc[:, 256 * k:256 * k + 256].bitcast(FP8X4),
+                scales=ws[:, 256 * k:256 * k + 256],
+                in_=wg[:, 2 * k:2 * k + 2, :, :].rearrange("p b o t -> p (b o t)"),
+            )
+
+        def w_group(ks):
+            for n, k in enumerate(ks):
+                w_transpose(k)
+                if n > 0:
+                    w_quant(ks[n - 1])
+            w_quant(ks[-1])
+
+        def x_norm(c, b2):
+            bp, hq = divmod(c, 4)
+            xf = xs[2 * bp + b2][:].bitcast(F32)
+            xt = tp.tile([P, 4, P], F32, name="xt", tag="tp")
+            for t in range(4):
+                nc.tensor.transpose(xt[:, t, :], xf[:, t, hq * P:(hq + 1) * P], ident_f[:])
+            xv = xt[:].bitcast(BF16).rearrange("p t (q par) -> p par t q", par=2)
+            for par in range(2):
+                junk = junkp.tile([P, 4, P], BF16, name="junk")
+                col = 4 * c + 2 * b2 + par
+                nc.scalar.activation(out=junk[:], in_=xv[:, par], func=ACT.Square,
+                                     accum_out=sm["n2"][:, col:col + 1])
+
+        def chain_in_a(c):
+            nc.gpsimd.tensor_scalar(out=s4("y4", c), in0=s4("n2", c), scalar1=0.04, scalar2=4e-16,
+                                    op0=ALU.mult, op1=ALU.max)
+            nc.gpsimd.tensor_tensor(out=s4("rzh", c), in0=s4("y4", c), in1=mhalf4[:], op=ALU.pow)
+            nc.gpsimd.tensor_tensor(out=s4("z2", c), in0=s4("y4", c), in1=s4("rzh", c), op=ALU.mult)
+            nc.gpsimd.tensor_scalar(out=s4("zc", c), in0=s4("z2", c), scalar1=0.5, scalar2=ZMAX,
+                                    op0=ALU.mult, op1=ALU.min)
+
+        def chain_in_b(c):
+            nc.scalar.activation(out=s4("la", c), in_=s4("zc", c), func=ACT.Ln, bias=ones1[:], scale=1.0)
+            nc.scalar.activation(out=s4("lb", c), in_=s4("zc", c), func=ACT.Ln, bias=ones1[:], scale=-1.0)
+            nc.gpsimd.tensor_tensor(out=s4("dd", c), in0=s4("la", c), in1=s4("lb", c), op=ALU.subtract)
+            nc.gpsimd.tensor_tensor(out=s4("gg", c), in0=s4("dd", c), in1=s4("rzh", c), op=ALU.mult)
+
+        g_banks = {}
+
+        def g_bcast(c):
+            gb = bc.tile([P, 4, P], F32, name="gb", tag="bc")
+            for k in range(4):
+                nc.tensor.transpose(gb[:, k, :], sm["gg"][:, 4 * c + k:4 * c + k + 1].to_broadcast([P, P]), ident_f[:])
+            g_banks[c] = gb
+
+        def u_stage(c, fill):
+            bp, hq = divmod(c, 4)
+            gb = g_banks[c]
+            uc = upool.tile([P, ROWS, 2, W, 4], BF16, name="uc", align_bytes=64)
+            for b2 in range(2):
+                in0 = xs[2 * bp + b2][:, :, hq * 256:(hq + 1) * 256].rearrange(
+                    "p t (h w2 par) -> p h w2 par t", h=ROWS, w2=16, par=2)
+                in1 = gb[:, 2 * b2:2 * b2 + 2, :].rearrange("p par (h w2) -> p h w2 par", h=ROWS)
+                in1 = in1.unsqueeze(4).to_broadcast([P, ROWS, 16, 2, 4])
+                o = uc[:, :, b2, :, :].rearrange("p h (w2 par) t -> p h w2 par t", par=2)
+                nc.vector.tensor_tensor(out=o, in0=in0, in1=in1, op=ALU.mult)
+            ucr = uc[:].rearrange("p h b w t -> p (h b) (w t)")
+            k = c % 2
+            lo = (ROWS * hq + 1) * 64
+            srcs = [ul[k][:].rearrange("p r c -> p (r c)"), uc[:].rearrange("p h b w t -> p (h b w t)"),
+                    ur[k][:].rearrange("p r c -> p (r c)")]
+
+            def quant(j):
+                nc.vector.quantize_mx(out=codes[j][bp][:, lo:lo + 512].bitcast(FP8X4),
+                                      scales=planes[j][bp][:, lo:lo + 512], in_=srcs[j])
+
+            if c < EARLY_COPY:
+                nc.vector.tensor_copy(out=ur[k][:, :, 0:124], in_=ucr[:, :, 4:128])
+            else:
+                nc.scalar.copy(out=ur[k][:, :, 0:124], in_=ucr[:, :, 4:128])
+            nc.vector.tensor_copy(out=ul[k][:, :, 4:128], in_=ucr[:, :, 0:124])
+            quant(1)
+            for f in fill[0]:
+                f()
+            quant(0)
+            quant(2)
+            for f in fill[1]:
+                f()
+
+        accs = {}
+        r_tiles = {}
+
+        def mx_passes(s, half, i_list, first, last):
+            bp, hq = divmod(s, 4)
+            if first:
+                acc_new = accp.tile([P, 512], F32, name="acc", tag="acc")
+                accs[(s, half)] = acc_new
+            acc = accs[(s, half)]
+            todo = [(i, j) for i in i_list for j in (1, 0, 2)]
+            for n, (i, j) in enumerate(todo):
+                blk = 2 * (3 * i + j) + half
+                lo = (ROWS * hq + i) * 64
+                nc.tensor.matmul_mx(
+                    out=acc[:],
+                    lhsT=wc[:, blk * P:(blk + 1) * P].bitcast(FP8X4),
+                    lhsT_scale=ws[:, blk * P:(blk + 1) * P],
+                    rhs=codes[j][bp][:, lo:lo + 512].bitcast(FP8X4),
+                    rhs_scale=planes[j][bp][:, lo:lo + 512],
+                    start=(first and n == 0), stop=(last and n == len(todo) - 1),
+                )
+
+        def relu(s, half):
+            r = rpool.tile([P, 512], F32, name="r")
+            if s < EARLY_RELU:
+                nc.vector.tensor_scalar(out=r[:], in0=accs[(s, half)][:], scalar1=bias_sb[:, half:half + 1], scalar2=0.0,
+                                        op0=ALU.add, op1=ALU.max)
+            else:
+                nc.scalar.activation(out=r[:], in_=accs[(s, half)][:], func=ACT.Relu,
+                                     bias=bias_sb[:, half:half + 1], scale=1.0)
+            r_tiles[(s, half)] = r
+
+        def out_norm(s, pg):
+            rt = tp.tile([P, 2, 2, P], F32, name="rt", tag="tp")
+            for pl in range(2):
+                pb = 2 * pg + pl
+                for half in range(2):
+                    nc.tensor.transpose(rt[:, pl, half, :], r_tiles[(s, half)][:, pb * P:(pb + 1) * P], ident_f[:])
+            for pl in range(2):
+                junk = junkp.tile([P, 2, P], BF16, name="junk2")
+                col = 4 * s + 2 * pg + pl
+                nc.scalar.activation(out=junk[:], in_=rt[:, pl], func=ACT.Square,
+                                     accum_out=sm["m2"][:, col:col + 1])
+
+        def chain_out_a(s):
+            nc.gpsimd.tensor_scalar(out=s4("y2o", s), in0=s4("m2", s), scalar1=0.01, scalar2=1e-16,
+                                    op0=ALU.mult, op1=ALU.max)
+            nc.gpsimd.tensor_tensor(out=s4("rzo", s), in0=s4("y2o", s), in1=mhalf4[:], op=ALU.pow)
+            nc.gpsimd.tensor_tensor(out=s4("zm", s), in0=s4("y2o", s), in1=s4("rzo", s), op=ALU.mult)
+
+        def chain_out_b(s):
+            nc.scalar.activation(out=s4("th", s), in_=s4("zm", s), func=ACT.Tanh)
+            nc.gpsimd.tensor_tensor(out=s4("tf", s), in0=s4("th", s), in1=s4("rzo", s), op=ALU.mult)
+
+        t_banks = {}
+
+        def t_bcast(s):
+            tb = bc.tile([P, 4, P], F32, name="tb", tag="bc")
+            for k in range(4):
+                nc.tensor.transpose(tb[:, k, :], sm["tf"][:, 4 * s + k:4 * s + k + 1].to_broadcast([P, P]), ident_f[:])
+            t_banks[s] = tb
+
+        def finish(s, half):
+            bp, hq = divmod(s, 4)
+            tv = t_banks[s][:].rearrange("p k (a b w) -> p (k a) b w", a=2, b=2)
+            ob = opool.tile([P, 2, ROWS, W], F32, name="ob")
+            rv = r_tiles[(s, half)][:].rearrange("p (h b w) -> p h b w", h=ROWS, b=2)
+            nc.vector.tensor_tensor(out=ob[:].rearrange("p b h w -> p h b w"), in0=rv, in1=tv, op=ALU.mult)
+            nc.sync.dma_start(
+                out=out[2 * bp:2 * bp + 2, half * P:(half + 1) * P, ROWS * hq:ROWS * hq + ROWS, :].rearrange(
+                    "b p h w -> p b (h w)"),
+                in_=ob[:].rearrange("p b h w -> p b (h w)"),
+            )
+
+        def nothing():
+            return None
+
+        def finisher(s, half):
+            if 0 <= s < NCH:
+                return lambda: finish(s, half)
+            return nothing
+
+        def x_chunk(c):
+            x_norm(c, 0)
+            if c > 0:
+                chain_in_b(c - 1)
+            x_norm(c, 1)
+            chain_in_a(c)
+
+        bt = tp.tile([P, P], BF16, name="bt", tag="tp")
+        nc.tensor.transpose(bt[:], btile[:], ident_b[:])
+        bias_sb = const.tile([P, 2], F32, name="bias_sb")
+        nc.vector.tensor_copy(out=bias_sb[:], in_=bt[:, 0:2])
+        x_chunk(0)
+        w_group([0, 1, 2])
+        x_chunk(1)
+        for k in (3, 4, 5):
+            w_transpose(k)
+        g_bcast(0)
+        for k in (6, 7, 8):
+            w_transpose(k)
+        u_stage(0, [[lambda: w_quant(3), lambda: w_quant(4)], [lambda: w_quant(5)]])
+        x_chunk(2)
+        for k in (6, 7, 8):
+            w_quant(k)
+
+        for c in range(NCH + 3):
+            if 1 <= c <= NCH and (c - 1) % 4 < 3:
+                for half in range(2):
+                    mx_passes(c - 1, half, [2], False, True)
+                    relu(c - 1, half)
+            if c < NCH:
+                closes = (c % 4 == 3)
+                mx_passes(c, 0, [0, 1, 2] if closes else [0, 1], True, closes)
+                if closes:
+                    relu(c, 0)
+                if c == 0:
+                    g_bcast(1)
+                if 2 * c + 3 < NCH:
+                    x_chunk(2 * c + 3)
+                mx_passes(c, 1, [0, 1, 2] if closes else [0, 1], True, closes)
+                if closes:
+                    relu(c, 1)
+            fins = [finisher(c - 3, half) for half in range(2)]
+            if c + 1 < NCH:
+                u_stage(c + 1, [fins[0:1], fins[1:]])
+            else:
+                for f in fins:
+                    f()
+            if c == 2:
+                chain_in_b(7)
+            if 0 <= c - 2 < NCH:
+                chain_out_b(c - 2)
+            if 0 <= c - 1 < NCH:
+                out_norm(c - 1, 0)
+                out_norm(c - 1, 1)
+                chain_out_a(c - 1)
+            if 0 <= c - 2 < NCH:
+                t_bcast(c - 2)
+            if c + 2 < NCH:
+                g_bcast(c + 2)
+            if 2 * c + 4 < NCH:
+                x_chunk(2 * c + 4)
+        finish(NCH - 1, 0)
+        finish(NCH - 1, 1)

@@ -31,8 +31,8 @@ def tile_pvconv2d_t_kernel(tc, x, Wk, bias, out):
         const = ctx.enter_context(tc.tile_pool(name="const", bufs=1))
         upool = ctx.enter_context(tc.tile_pool(name="upool", bufs=2))
         junkp = ctx.enter_context(tc.tile_pool(name="junkp", bufs=2))
-        rpool = ctx.enter_context(tc.tile_pool(name="rpool", bufs=10))
-        opool = ctx.enter_context(tc.tile_pool(name="opool", bufs=4))
+        rpool = ctx.enter_context(tc.tile_pool(name="rpool", bufs=12))
+        opool = ctx.enter_context(tc.tile_pool(name="opool", bufs=6))
         tp = ctx.enter_context(tc.psum_pool(name="tp", bufs=TP_BUFS))
         bc = ctx.enter_context(tc.psum_pool(name="bc", bufs=BC_BUFS))
         accp = ctx.enter_context(tc.psum_pool(name="accp", bufs=ACC_BUFS))
@@ -189,12 +189,12 @@ def tile_pvconv2d_t_kernel(tc, x, Wk, bias, out):
                 nc.vector.quantize_mx(out=codes[j][bp][:, lo:lo + 512].bitcast(FP8X4),
                                       scales=planes[j][bp][:, lo:lo + 512], in_=srcs[j])
 
+            if c >= EARLY_COPY:
+                nc.scalar.copy(out=ur[k][:, :, 0:124], in_=ucr[:, :, 4:128])
+            quant(1)
+            nc.vector.tensor_copy(out=ul[k][:, :, 4:128], in_=ucr[:, :, 0:124])
             if c < EARLY_COPY:
                 nc.vector.tensor_copy(out=ur[k][:, :, 0:124], in_=ucr[:, :, 4:128])
-            else:
-                nc.scalar.copy(out=ur[k][:, :, 0:124], in_=ucr[:, :, 4:128])
-            nc.vector.tensor_copy(out=ul[k][:, :, 4:128], in_=ucr[:, :, 0:124])
-            quant(1)
             for f in fill[0]:
                 f()
             quant(0)
@@ -211,7 +211,7 @@ def tile_pvconv2d_t_kernel(tc, x, Wk, bias, out):
                 acc_new = accp.tile([P, 512], F32, name="acc", tag="acc")
                 accs[(s, half)] = acc_new
             acc = accs[(s, half)]
-            todo = [(i, j) for i in i_list for j in (1, 0, 2)]
+            todo = [(i, j) for j in (1, 0, 2) for i in i_list]
             for n, (i, j) in enumerate(todo):
                 blk = 2 * (3 * i + j) + half
                 lo = (ROWS * hq + i) * 64
@@ -296,36 +296,52 @@ def tile_pvconv2d_t_kernel(tc, x, Wk, bias, out):
         bias_sb = const.tile([P, 2], F32, name="bias_sb")
         nc.vector.tensor_copy(out=bias_sb[:], in_=bt[:, 0:2])
         x_chunk(0)
-        w_group([0, 1, 2])
         x_chunk(1)
+        w_group([0, 1, 2])
+        g_bcast(0)
         for k in (3, 4, 5):
             w_transpose(k)
-        g_bcast(0)
+        chain_in_b(1)
         for k in (6, 7, 8):
             w_transpose(k)
         u_stage(0, [[lambda: w_quant(3), lambda: w_quant(4)], [lambda: w_quant(5)]])
-        x_chunk(2)
+        g_bcast(1)
+        x_norm(2, 0)
+        x_norm(2, 1)
+        chain_in_a(2)
         for k in (6, 7, 8):
             w_quant(k)
 
-        for c in range(NCH + 3):
+        def tanh_step(s):
+            return s + 3 if s < 4 else s + 2
+
+        def tile_norm(s):
+            out_norm(s, 0)
+            out_norm(s, 1)
+            chain_out_a(s)
+
+        for c in range(NCH + 4):
             if 1 <= c <= NCH and (c - 1) % 4 < 3:
                 for half in range(2):
                     mx_passes(c - 1, half, [2], False, True)
                     relu(c - 1, half)
+            ready = [s for s in range(NCH) if tanh_step(s) == c]
+            mid = (False) and c < NCH
             if c < NCH:
+                for s in ready:
+                    chain_out_b(s)
                 closes = (c % 4 == 3)
                 mx_passes(c, 0, [0, 1, 2] if closes else [0, 1], True, closes)
                 if closes:
                     relu(c, 0)
-                if c == 0:
-                    g_bcast(1)
+                if mid:
+                    tile_norm(c - 1)
                 if 2 * c + 3 < NCH:
                     x_chunk(2 * c + 3)
                 mx_passes(c, 1, [0, 1, 2] if closes else [0, 1], True, closes)
                 if closes:
                     relu(c, 1)
-            fins = [finisher(c - 3, half) for half in range(2)]
+            fins = [finisher(s, half) for s in range(NCH) if tanh_step(s) + 1 == c for half in range(2)]
             if c + 1 < NCH:
                 u_stage(c + 1, [fins[0:1], fins[1:]])
             else:
@@ -333,17 +349,14 @@ def tile_pvconv2d_t_kernel(tc, x, Wk, bias, out):
                     f()
             if c == 2:
                 chain_in_b(7)
-            if 0 <= c - 2 < NCH:
-                chain_out_b(c - 2)
-            if 0 <= c - 1 < NCH:
-                out_norm(c - 1, 0)
-                out_norm(c - 1, 1)
-                chain_out_a(c - 1)
-            if 0 <= c - 2 < NCH:
-                t_bcast(c - 2)
+            if 0 <= c - 1 < NCH and not mid:
+                tile_norm(c - 1)
+            if c >= NCH:
+                for s in ready:
+                    chain_out_b(s)
             if c + 2 < NCH:
                 g_bcast(c + 2)
+            for s in ready:
+                t_bcast(s)
             if 2 * c + 4 < NCH:
                 x_chunk(2 * c + 4)
-        finish(NCH - 1, 0)
-        finish(NCH - 1, 1)

@@ -20,8 +20,8 @@ ROWS = 8
 NCH = 8
 PADW = (H + 2) * 64
 ACC_BUFS, TP_BUFS, BC_BUFS = 3, 2, 3
-EARLY_RELU = 2
-EARLY_COPY = 4
+EARLY_RELU = 0
+EARLY_COPY = 0
 
 
 def tile_pvconv2d_t_kernel(tc, x, Wk, bias, out):

@@ -27,7 +27,6 @@ EARLY_COPY = 0
 def tile_pvconv2d_t_kernel(tc, x, Wk, bias, out):
     nc = tc.nc
     with ExitStack() as ctx:
-        ctx.enter_context(tc.manual_schedule())
         const = ctx.enter_context(tc.tile_pool(name="const", bufs=1))
         upool = ctx.enter_context(tc.tile_pool(name="upool", bufs=2))
         junkp = ctx.enter_context(tc.tile_pool(name="junkp", bufs=2))

@@ -27,8 +27,9 @@ EARLY_COPY = 0
 def tile_pvconv2d_t_kernel(tc, x, Wk, bias, out):
     nc = tc.nc
     with ExitStack() as ctx:
+        ctx.enter_context(tc.manual_schedule())
         const = ctx.enter_context(tc.tile_pool(name="const", bufs=1))
-        upool = ctx.enter_context(tc.tile_pool(name="upool", bufs=2))
+        upool = ctx.enter_context(tc.tile_pool(name="upool", bufs=3))
         junkp = ctx.enter_context(tc.tile_pool(name="junkp", bufs=2))
         rpool = ctx.enter_context(tc.tile_pool(name="rpool", bufs=12))
         opool = ctx.enter_context(tc.tile_pool(name="opool", bufs=6))
@@ -55,9 +56,6 @@ def tile_pvconv2d_t_kernel(tc, x, Wk, bias, out):
         planes = [[const.tile([P, PADW], U8, name="planes%d%d" % (j, bp), align_bytes=64) for bp in range(2)] for j in range(3)]
         ul = [const.tile([P, 16, 128], BF16, name="ul%d" % k, align_bytes=64) for k in range(2)]
         ur = [const.tile([P, 16, 128], BF16, name="ur%d" % k, align_bytes=64) for k in range(2)]
-        for k in range(2):
-            nc.vector.memset(ul[k][:, :, 0:4], 0.0)
-            nc.scalar.copy(out=ur[k][:, :, 124:128], in_=zeros[:])
         for j in range(3):
             for bp in range(2):
                 for lo in (0, PADW - 64):
@@ -178,27 +176,27 @@ def tile_pvconv2d_t_kernel(tc, x, Wk, bias, out):
                 in1 = in1.unsqueeze(4).to_broadcast([P, ROWS, 16, 2, 4])
                 o = uc[:, :, b2, :, :].rearrange("p h (w2 par) t -> p h w2 par t", par=2)
                 nc.vector.tensor_tensor(out=o, in0=in0, in1=in1, op=ALU.mult)
-            ucr = uc[:].rearrange("p h b w t -> p (h b) (w t)")
+            ucf = uc[:].rearrange("p h b w t -> p (h b w t)")
             k = c % 2
-            lo = (ROWS * hq + 1) * 64
-            srcs = [ul[k][:].rearrange("p r c -> p (r c)"), uc[:].rearrange("p h b w t -> p (h b w t)"),
-                    ur[k][:].rearrange("p r c -> p (r c)")]
-
-            def quant(j):
-                nc.vector.quantize_mx(out=codes[j][bp][:, lo:lo + 512].bitcast(FP8X4),
-                                      scales=planes[j][bp][:, lo:lo + 512], in_=srcs[j])
-
-            if c >= EARLY_COPY:
-                nc.scalar.copy(out=ur[k][:, :, 0:124], in_=ucr[:, :, 4:128])
-            quant(1)
-            nc.vector.tensor_copy(out=ul[k][:, :, 4:128], in_=ucr[:, :, 0:124])
-            if c < EARLY_COPY:
-                nc.vector.tensor_copy(out=ur[k][:, :, 0:124], in_=ucr[:, :, 4:128])
+            nc.sync.dma_start(out=ul[k][:].rearrange("p r c -> p (r c)")[:, 4:2048], in_=ucf[:, 0:2044])
+            nc.sync.dma_start(out=ur[k][:].rearrange("p r c -> p (r c)")[:, 0:2044], in_=ucf[:, 4:2048])
+            quant(c, 1, ucf)
             for f in fill[0]:
                 f()
-            quant(0)
-            quant(2)
-            for f in fill[1]:
+
+        def quant(c, j, src):
+            bp, hq = divmod(c, 4)
+            lo = (ROWS * hq + 1) * 64
+            nc.vector.quantize_mx(out=codes[j][bp][:, lo:lo + 512].bitcast(FP8X4),
+                                  scales=planes[j][bp][:, lo:lo + 512], in_=src)
+
+        def u_back(c, fill):
+            k = c % 2
+            nc.vector.memset(ul[k][:, :, 0:4], 0.0)
+            nc.vector.memset(ur[k][:, :, 124:128], 0.0)
+            quant(c, 0, ul[k][:].rearrange("p r c -> p (r c)"))
+            quant(c, 2, ur[k][:].rearrange("p r c -> p (r c)"))
+            for f in fill:
                 f()
 
         accs = {}
@@ -303,13 +301,15 @@ def tile_pvconv2d_t_kernel(tc, x, Wk, bias, out):
         chain_in_b(1)
         for k in (6, 7, 8):
             w_transpose(k)
-        u_stage(0, [[lambda: w_quant(3), lambda: w_quant(4)], [lambda: w_quant(5)]])
+        u_stage(0, [[lambda: w_quant(3), lambda: w_quant(4), lambda: w_quant(5)]])
         g_bcast(1)
         x_norm(2, 0)
         x_norm(2, 1)
         chain_in_a(2)
-        for k in (6, 7, 8):
-            w_quant(k)
+        u_stage(1, [[]])
+        u_back(0, [lambda: w_quant(6), lambda: w_quant(7), lambda: w_quant(8)])
+        x_chunk(3)
+        g_bcast(2)
 
         def tanh_step(s):
             return s + 3 if s < 4 else s + 2
@@ -325,7 +325,6 @@ def tile_pvconv2d_t_kernel(tc, x, Wk, bias, out):
                     mx_passes(c - 1, half, [2], False, True)
                     relu(c - 1, half)
             ready = [s for s in range(NCH) if tanh_step(s) == c]
-            mid = (False) and c < NCH
             if c < NCH:
                 for s in ready:
                     chain_out_b(s)
@@ -333,29 +332,30 @@ def tile_pvconv2d_t_kernel(tc, x, Wk, bias, out):
                 mx_passes(c, 0, [0, 1, 2] if closes else [0, 1], True, closes)
                 if closes:
                     relu(c, 0)
-                if mid:
-                    tile_norm(c - 1)
-                if 2 * c + 3 < NCH:
-                    x_chunk(2 * c + 3)
+                if 2 * c + 4 < NCH:
+                    x_chunk(2 * c + 4)
                 mx_passes(c, 1, [0, 1, 2] if closes else [0, 1], True, closes)
                 if closes:
                     relu(c, 1)
             fins = [finisher(s, half) for s in range(NCH) if tanh_step(s) + 1 == c for half in range(2)]
+            if c + 2 < NCH:
+                u_stage(c + 2, [fins[0:1]])
+                fins = fins[1:]
             if c + 1 < NCH:
-                u_stage(c + 1, [fins[0:1], fins[1:]])
+                u_back(c + 1, fins)
             else:
                 for f in fins:
                     f()
             if c == 2:
                 chain_in_b(7)
-            if 0 <= c - 1 < NCH and not mid:
+            if 0 <= c - 1 < NCH:
                 tile_norm(c - 1)
             if c >= NCH:
                 for s in ready:
                     chain_out_b(s)
-            if c + 2 < NCH:
-                g_bcast(c + 2)
+            if c + 3 < NCH:
+                g_bcast(c + 3)
             for s in ready:
                 t_bcast(s)
-            if 2 * c + 4 < NCH:
-                x_chunk(2 * c + 4)
+            if 2 * c + 5 < NCH:
+                x_chunk(2 * c + 5)

@@ -15,13 +15,13 @@ ACT = mybir.ActivationFunctionType
 P = 128
 B, C, O, H, W = 4, 512, 256, 32, 32
 FLOPS = 2 * B * H * W * C * 9 * O
-ZMAX = 1.0 - 1e-6
+Z_MAX = 1.0 - 1e-6
 ROWS = 8
-NCH = 8
-PADW = (H + 2) * 64
-ACC_BUFS, TP_BUFS, BC_BUFS = 3, 2, 3
-EARLY_RELU = 0
-EARLY_COPY = 0
+PITCH = 64
+N_TILE = ROWS * PITCH
+N_CHUNKS = 8
+PAIR_COLS = (H + 2) * PITCH
+N_BLOCKS = 18
 
 
 def tile_pvconv2d_t_kernel(tc, x, Wk, bias, out):
@@ -29,13 +29,13 @@ def tile_pvconv2d_t_kernel(tc, x, Wk, bias, out):
     with ExitStack() as ctx:
         ctx.enter_context(tc.manual_schedule())
         const = ctx.enter_context(tc.tile_pool(name="const", bufs=1))
-        upool = ctx.enter_context(tc.tile_pool(name="upool", bufs=3))
+        upool = ctx.enter_context(tc.tile_pool(name="upool", bufs=2))
         junkp = ctx.enter_context(tc.tile_pool(name="junkp", bufs=2))
         rpool = ctx.enter_context(tc.tile_pool(name="rpool", bufs=12))
         opool = ctx.enter_context(tc.tile_pool(name="opool", bufs=6))
-        tp = ctx.enter_context(tc.psum_pool(name="tp", bufs=TP_BUFS))
-        bc = ctx.enter_context(tc.psum_pool(name="bc", bufs=BC_BUFS))
-        accp = ctx.enter_context(tc.psum_pool(name="accp", bufs=ACC_BUFS))
+        tp = ctx.enter_context(tc.psum_pool(name="tp", bufs=2))
+        bc = ctx.enter_context(tc.psum_pool(name="bc", bufs=3))
+        accp = ctx.enter_context(tc.psum_pool(name="accp", bufs=3))
 
         ident_f = const.tile([P, P], F32, name="ident_f")
         make_identity(nc, ident_f[:])
@@ -52,31 +52,30 @@ def tile_pvconv2d_t_kernel(tc, x, Wk, bias, out):
         btile = const.tile([P, P], BF16, name="btile")
         nc.vector.memset(btile[:], 0.0)
 
-        codes = [[const.tile([P, PADW], U32, name="codes%d%d" % (j, bp), align_bytes=64) for bp in range(2)] for j in range(3)]
-        planes = [[const.tile([P, PADW], U8, name="planes%d%d" % (j, bp), align_bytes=64) for bp in range(2)] for j in range(3)]
-        ul = [const.tile([P, 16, 128], BF16, name="ul%d" % k, align_bytes=64) for k in range(2)]
-        ur = [const.tile([P, 16, 128], BF16, name="ur%d" % k, align_bytes=64) for k in range(2)]
+        codes = [[const.tile([P, PAIR_COLS], U32, name="codes%d%d" % (j, pair), align_bytes=64) for pair in range(2)]
+                 for j in range(3)]
+        planes = [[const.tile([P, PAIR_COLS], U8, name="planes%d%d" % (j, pair), align_bytes=64) for pair in range(2)]
+                  for j in range(3)]
+        u_right = [const.tile([P, 16, 128], BF16, name="ul%d" % k, align_bytes=64) for k in range(2)]
+        u_left = [const.tile([P, 16, 128], BF16, name="ur%d" % k, align_bytes=64) for k in range(2)]
+        for k in range(2):
+            nc.vector.memset(u_right[k][:, :, 0:4], 0.0)
+            nc.scalar.copy(out=u_left[k][:, :, 124:128], in_=zeros[:])
         for j in range(3):
-            for bp in range(2):
-                for lo in (0, PADW - 64):
-                    nc.vector.memset(codes[j][bp][:, lo:lo + 64].bitcast(I32), 0)
-                    nc.vector.memset(planes[j][bp][:, lo:lo + 64].bitcast(I32), 0)
+            for pair in range(2):
+                for lo in (0, PAIR_COLS - PITCH):
+                    nc.vector.memset(codes[j][pair][:, lo:lo + PITCH].bitcast(I32), 0)
+                    nc.vector.memset(planes[j][pair][:, lo:lo + PITCH].bitcast(I32), 0)
 
         names = ["n2", "y4", "z2", "zc", "la", "lb", "rzh", "dd", "gg", "m2", "y2o", "zm", "th", "rzo", "tf"]
-        sm = dict((nm, const.tile([P, 4 * NCH], F32, name="sm_" + nm)) for nm in names)
+        sm = dict((nm, const.tile([P, 4 * N_CHUNKS], F32, name="sm_" + nm)) for nm in names)
 
-        def s4(nm, c):
+        def compact(nm, c):
             return sm[nm][:, 4 * c:4 * c + 4]
 
         xs = [const.tile([P, 4, H * W], BF16, name="xs%d" % b) for b in range(B)]
-        w_sb = const.tile([P, 18, C], BF16, name="w_sb")
+        w_sb = const.tile([P, N_BLOCKS, C], BF16, name="w_sb")
         wk_v = Wk.rearrange("k (h p) c -> p (k h) c", p=P)
-
-        def load_x(b):
-            nc.sync.dma_start(
-                out=xs[b][:].rearrange("q (u e) n -> q u (e n)", u=2),
-                in_=x[b].rearrange("(u q e) h w -> q u (e h w)", u=2, q=P, e=2),
-            )
 
         def load_x_half(b, hh):
             xv = x[b].rearrange("(u q e) h w -> u q e (h w)", u=2, q=P, e=2)
@@ -84,25 +83,21 @@ def tile_pvconv2d_t_kernel(tc, x, Wk, bias, out):
                 nc.sync.dma_start(out=xs[b][:, 2 * u:2 * u + 2, hh * 512:(hh + 1) * 512],
                                   in_=xv[u][:, :, hh * 512:(hh + 1) * 512])
 
-        def load_w(k3):
-            nc.sync.dma_start(out=w_sb[:, 6 * k3:6 * k3 + 6, :], in_=wk_v[:, 6 * k3:6 * k3 + 6, :])
+        def load_w(kernel_row):
+            nc.sync.dma_start(out=w_sb[:, 6 * kernel_row:6 * kernel_row + 6, :],
+                              in_=wk_v[:, 6 * kernel_row:6 * kernel_row + 6, :])
 
         nc.scalar.dma_start(out=btile[0:2, :], in_=bias.rearrange("(h o) -> h o", h=2))
         load_x_half(0, 0)
         load_x_half(1, 0)
-        load_w(0)
-        load_w(1)
-        load_w(2)
-        load_x_half(0, 1)
-        load_x_half(1, 1)
-        load_x_half(2, 0)
-        load_x_half(3, 0)
-        load_x_half(2, 1)
-        load_x_half(3, 1)
+        for kernel_row in range(3):
+            load_w(kernel_row)
+        for b, hh in ((0, 1), (1, 1), (2, 0), (3, 0), (2, 1), (3, 1)):
+            load_x_half(b, hh)
 
-        wg = const.tile([P, 18, P, 4], BF16, name="wg", align_bytes=64)
-        wc = const.tile([P, 18 * P], U32, name="wc", align_bytes=64)
-        ws = const.tile([P, 18 * P], U8, name="ws", align_bytes=64)
+        wg = const.tile([P, N_BLOCKS, P, 4], BF16, name="wg", align_bytes=64)
+        wc = const.tile([P, N_BLOCKS * P], U32, name="wc", align_bytes=64)
+        ws = const.tile([P, N_BLOCKS * P], U8, name="ws", align_bytes=64)
         w_f = w_sb[:].bitcast(F32)
         wg_f = wg[:].bitcast(F32)
 
@@ -111,10 +106,8 @@ def tile_pvconv2d_t_kernel(tc, x, Wk, bias, out):
             for bl in range(2):
                 for u in range(2):
                     nc.tensor.transpose(wt[:, bl, u, :], w_f[:, 2 * k + bl, u * P:(u + 1) * P], ident_f[:])
-            if k < 3:
-                nc.vector.tensor_copy(out=wg_f[:, 2 * k:2 * k + 2, :, :], in_=wt[:].rearrange("p b u o -> p b o u"))
-            else:
-                nc.scalar.copy(out=wg_f[:, 2 * k:2 * k + 2, :, :], in_=wt[:].rearrange("p b u o -> p b o u"))
+            copy = nc.vector.tensor_copy if k < 3 else nc.scalar.copy
+            copy(out=wg_f[:, 2 * k:2 * k + 2, :, :], in_=wt[:].rearrange("p b u o -> p b o u"))
 
         def w_quant(k):
             nc.vector.quantize_mx(
@@ -123,16 +116,9 @@ def tile_pvconv2d_t_kernel(tc, x, Wk, bias, out):
                 in_=wg[:, 2 * k:2 * k + 2, :, :].rearrange("p b o t -> p (b o t)"),
             )
 
-        def w_group(ks):
-            for n, k in enumerate(ks):
-                w_transpose(k)
-                if n > 0:
-                    w_quant(ks[n - 1])
-            w_quant(ks[-1])
-
         def x_norm(c, b2):
-            bp, hq = divmod(c, 4)
-            xf = xs[2 * bp + b2][:].bitcast(F32)
+            pair, hq = divmod(c, 4)
+            xf = xs[2 * pair + b2][:].bitcast(F32)
             xt = tp.tile([P, 4, P], F32, name="xt", tag="tp")
             for t in range(4):
                 nc.tensor.transpose(xt[:, t, :], xf[:, t, hq * P:(hq + 1) * P], ident_f[:])
@@ -143,92 +129,92 @@ def tile_pvconv2d_t_kernel(tc, x, Wk, bias, out):
                 nc.scalar.activation(out=junk[:], in_=xv[:, par], func=ACT.Square,
                                      accum_out=sm["n2"][:, col:col + 1])
 
-        def chain_in_a(c):
-            nc.gpsimd.tensor_scalar(out=s4("y4", c), in0=s4("n2", c), scalar1=0.04, scalar2=4e-16,
+        def x_root(c):
+            nc.gpsimd.tensor_scalar(out=compact("y4", c), in0=compact("n2", c), scalar1=0.04, scalar2=4e-16,
                                     op0=ALU.mult, op1=ALU.max)
-            nc.gpsimd.tensor_tensor(out=s4("rzh", c), in0=s4("y4", c), in1=mhalf4[:], op=ALU.pow)
-            nc.gpsimd.tensor_tensor(out=s4("z2", c), in0=s4("y4", c), in1=s4("rzh", c), op=ALU.mult)
-            nc.gpsimd.tensor_scalar(out=s4("zc", c), in0=s4("z2", c), scalar1=0.5, scalar2=ZMAX,
+            nc.gpsimd.tensor_tensor(out=compact("rzh", c), in0=compact("y4", c), in1=mhalf4[:], op=ALU.pow)
+            nc.gpsimd.tensor_tensor(out=compact("z2", c), in0=compact("y4", c), in1=compact("rzh", c), op=ALU.mult)
+            nc.gpsimd.tensor_scalar(out=compact("zc", c), in0=compact("z2", c), scalar1=0.5, scalar2=Z_MAX,
                                     op0=ALU.mult, op1=ALU.min)
 
-        def chain_in_b(c):
-            nc.scalar.activation(out=s4("la", c), in_=s4("zc", c), func=ACT.Ln, bias=ones1[:], scale=1.0)
-            nc.scalar.activation(out=s4("lb", c), in_=s4("zc", c), func=ACT.Ln, bias=ones1[:], scale=-1.0)
-            nc.gpsimd.tensor_tensor(out=s4("dd", c), in0=s4("la", c), in1=s4("lb", c), op=ALU.subtract)
-            nc.gpsimd.tensor_tensor(out=s4("gg", c), in0=s4("dd", c), in1=s4("rzh", c), op=ALU.mult)
+        def x_factor(c):
+            nc.scalar.activation(out=compact("la", c), in_=compact("zc", c), func=ACT.Ln, bias=ones1[:], scale=1.0)
+            nc.scalar.activation(out=compact("lb", c), in_=compact("zc", c), func=ACT.Ln, bias=ones1[:], scale=-1.0)
+            nc.gpsimd.tensor_tensor(out=compact("dd", c), in0=compact("la", c), in1=compact("lb", c), op=ALU.subtract)
+            nc.gpsimd.tensor_tensor(out=compact("gg", c), in0=compact("dd", c), in1=compact("rzh", c), op=ALU.mult)
+
+        def x_chunk(c):
+            x_norm(c, 0)
+            if c > 0:
+                x_factor(c - 1)
+            x_norm(c, 1)
+            x_root(c)
 
         g_banks = {}
 
-        def g_bcast(c):
+        def g_spread(c):
             gb = bc.tile([P, 4, P], F32, name="gb", tag="bc")
             for k in range(4):
                 nc.tensor.transpose(gb[:, k, :], sm["gg"][:, 4 * c + k:4 * c + k + 1].to_broadcast([P, P]), ident_f[:])
             g_banks[c] = gb
 
-        def u_stage(c, fill):
-            bp, hq = divmod(c, 4)
+        def u_stage(c, fill_a, fill_b):
+            pair, hq = divmod(c, 4)
             gb = g_banks[c]
             uc = upool.tile([P, ROWS, 2, W, 4], BF16, name="uc", align_bytes=64)
             for b2 in range(2):
-                in0 = xs[2 * bp + b2][:, :, hq * 256:(hq + 1) * 256].rearrange(
+                in0 = xs[2 * pair + b2][:, :, hq * 256:(hq + 1) * 256].rearrange(
                     "p t (h w2 par) -> p h w2 par t", h=ROWS, w2=16, par=2)
                 in1 = gb[:, 2 * b2:2 * b2 + 2, :].rearrange("p par (h w2) -> p h w2 par", h=ROWS)
                 in1 = in1.unsqueeze(4).to_broadcast([P, ROWS, 16, 2, 4])
                 o = uc[:, :, b2, :, :].rearrange("p h (w2 par) t -> p h w2 par t", par=2)
                 nc.vector.tensor_tensor(out=o, in0=in0, in1=in1, op=ALU.mult)
-            ucf = uc[:].rearrange("p h b w t -> p (h b w t)")
+            rows = uc[:].rearrange("p h b w t -> p (h b) (w t)")
             k = c % 2
-            nc.sync.dma_start(out=ul[k][:].rearrange("p r c -> p (r c)")[:, 4:2048], in_=ucf[:, 0:2044])
-            nc.sync.dma_start(out=ur[k][:].rearrange("p r c -> p (r c)")[:, 0:2044], in_=ucf[:, 4:2048])
-            quant(c, 1, ucf)
-            for f in fill[0]:
-                f()
+            lo = (ROWS * hq + 1) * PITCH
+            sources = [u_right[k][:].rearrange("p r c -> p (r c)"), uc[:].rearrange("p h b w t -> p (h b w t)"),
+                       u_left[k][:].rearrange("p r c -> p (r c)")]
 
-        def quant(c, j, src):
-            bp, hq = divmod(c, 4)
-            lo = (ROWS * hq + 1) * 64
-            nc.vector.quantize_mx(out=codes[j][bp][:, lo:lo + 512].bitcast(FP8X4),
-                                  scales=planes[j][bp][:, lo:lo + 512], in_=src)
+            def quant(j):
+                nc.vector.quantize_mx(out=codes[j][pair][:, lo:lo + N_TILE].bitcast(FP8X4),
+                                      scales=planes[j][pair][:, lo:lo + N_TILE], in_=sources[j])
 
-        def u_back(c, fill):
-            k = c % 2
-            nc.vector.memset(ul[k][:, :, 0:4], 0.0)
-            nc.vector.memset(ur[k][:, :, 124:128], 0.0)
-            quant(c, 0, ul[k][:].rearrange("p r c -> p (r c)"))
-            quant(c, 2, ur[k][:].rearrange("p r c -> p (r c)"))
-            for f in fill:
-                f()
+            nc.scalar.copy(out=u_left[k][:, :, 0:124], in_=rows[:, :, 4:128])
+            nc.vector.tensor_copy(out=u_right[k][:, :, 4:128], in_=rows[:, :, 0:124])
+            for piece in fill_a:
+                piece()
+            quant(1)
+            quant(0)
+            quant(2)
+            for piece in fill_b:
+                piece()
 
         accs = {}
         r_tiles = {}
 
-        def mx_passes(s, half, i_list, first, last):
-            bp, hq = divmod(s, 4)
+        def mx_passes(s, half, kernel_rows, first, last):
+            pair, hq = divmod(s, 4)
             if first:
-                acc_new = accp.tile([P, 512], F32, name="acc", tag="acc")
+                acc_new = accp.tile([P, N_TILE], F32, name="acc", tag="acc")
                 accs[(s, half)] = acc_new
             acc = accs[(s, half)]
-            todo = [(i, j) for j in (1, 0, 2) for i in i_list]
+            todo = [(i, j) for j in (1, 0, 2) for i in kernel_rows]
             for n, (i, j) in enumerate(todo):
                 blk = 2 * (3 * i + j) + half
-                lo = (ROWS * hq + i) * 64
+                lo = (ROWS * hq + i) * PITCH
                 nc.tensor.matmul_mx(
                     out=acc[:],
                     lhsT=wc[:, blk * P:(blk + 1) * P].bitcast(FP8X4),
                     lhsT_scale=ws[:, blk * P:(blk + 1) * P],
-                    rhs=codes[j][bp][:, lo:lo + 512].bitcast(FP8X4),
-                    rhs_scale=planes[j][bp][:, lo:lo + 512],
+                    rhs=codes[j][pair][:, lo:lo + N_TILE].bitcast(FP8X4),
+                    rhs_scale=planes[j][pair][:, lo:lo + N_TILE],
                     start=(first and n == 0), stop=(last and n == len(todo) - 1),
                 )
 
         def relu(s, half):
-            r = rpool.tile([P, 512], F32, name="r")
-            if s < EARLY_RELU:
-                nc.vector.tensor_scalar(out=r[:], in0=accs[(s, half)][:], scalar1=bias_sb[:, half:half + 1], scalar2=0.0,
-                                        op0=ALU.add, op1=ALU.max)
-            else:
-                nc.scalar.activation(out=r[:], in_=accs[(s, half)][:], func=ACT.Relu,
-                                     bias=bias_sb[:, half:half + 1], scale=1.0)
+            r = rpool.tile([P, N_TILE], F32, name="r")
+            nc.scalar.activation(out=r[:], in_=accs[(s, half)][:], func=ACT.Relu,
+                                 bias=bias_sb[:, half:half + 1], scale=1.0)
             r_tiles[(s, half)] = r
 
         def out_norm(s, pg):
@@ -243,50 +229,37 @@ def tile_pvconv2d_t_kernel(tc, x, Wk, bias, out):
                 nc.scalar.activation(out=junk[:], in_=rt[:, pl], func=ACT.Square,
                                      accum_out=sm["m2"][:, col:col + 1])
 
-        def chain_out_a(s):
-            nc.gpsimd.tensor_scalar(out=s4("y2o", s), in0=s4("m2", s), scalar1=0.01, scalar2=1e-16,
+        def tile_norm(s):
+            out_norm(s, 0)
+            out_norm(s, 1)
+            nc.gpsimd.tensor_scalar(out=compact("y2o", s), in0=compact("m2", s), scalar1=0.01, scalar2=1e-16,
                                     op0=ALU.mult, op1=ALU.max)
-            nc.gpsimd.tensor_tensor(out=s4("rzo", s), in0=s4("y2o", s), in1=mhalf4[:], op=ALU.pow)
-            nc.gpsimd.tensor_tensor(out=s4("zm", s), in0=s4("y2o", s), in1=s4("rzo", s), op=ALU.mult)
+            nc.gpsimd.tensor_tensor(out=compact("rzo", s), in0=compact("y2o", s), in1=mhalf4[:], op=ALU.pow)
+            nc.gpsimd.tensor_tensor(out=compact("zm", s), in0=compact("y2o", s), in1=compact("rzo", s), op=ALU.mult)
 
-        def chain_out_b(s):
-            nc.scalar.activation(out=s4("th", s), in_=s4("zm", s), func=ACT.Tanh)
-            nc.gpsimd.tensor_tensor(out=s4("tf", s), in0=s4("th", s), in1=s4("rzo", s), op=ALU.mult)
+        def tile_factor(s):
+            nc.scalar.activation(out=compact("th", s), in_=compact("zm", s), func=ACT.Tanh)
+            nc.gpsimd.tensor_tensor(out=compact("tf", s), in0=compact("th", s), in1=compact("rzo", s), op=ALU.mult)
 
         t_banks = {}
 
-        def t_bcast(s):
+        def t_spread(s):
             tb = bc.tile([P, 4, P], F32, name="tb", tag="bc")
             for k in range(4):
                 nc.tensor.transpose(tb[:, k, :], sm["tf"][:, 4 * s + k:4 * s + k + 1].to_broadcast([P, P]), ident_f[:])
             t_banks[s] = tb
 
         def finish(s, half):
-            bp, hq = divmod(s, 4)
+            pair, hq = divmod(s, 4)
             tv = t_banks[s][:].rearrange("p k (a b w) -> p (k a) b w", a=2, b=2)
             ob = opool.tile([P, 2, ROWS, W], F32, name="ob")
             rv = r_tiles[(s, half)][:].rearrange("p (h b w) -> p h b w", h=ROWS, b=2)
             nc.vector.tensor_tensor(out=ob[:].rearrange("p b h w -> p h b w"), in0=rv, in1=tv, op=ALU.mult)
             nc.sync.dma_start(
-                out=out[2 * bp:2 * bp + 2, half * P:(half + 1) * P, ROWS * hq:ROWS * hq + ROWS, :].rearrange(
+                out=out[2 * pair:2 * pair + 2, half * P:(half + 1) * P, ROWS * hq:ROWS * hq + ROWS, :].rearrange(
                     "b p h w -> p b (h w)"),
                 in_=ob[:].rearrange("p b h w -> p b (h w)"),
             )
-
-        def nothing():
-            return None
-
-        def finisher(s, half):
-            if 0 <= s < NCH:
-                return lambda: finish(s, half)
-            return nothing
-
-        def x_chunk(c):
-            x_norm(c, 0)
-            if c > 0:
-                chain_in_b(c - 1)
-            x_norm(c, 1)
-            chain_in_a(c)
 
         bt = tp.tile([P, P], BF16, name="bt", tag="tp")
         nc.tensor.transpose(bt[:], btile[:], ident_b[:])
@@ -294,68 +267,65 @@ def tile_pvconv2d_t_kernel(tc, x, Wk, bias, out):
         nc.vector.tensor_copy(out=bias_sb[:], in_=bt[:, 0:2])
         x_chunk(0)
         x_chunk(1)
-        w_group([0, 1, 2])
-        g_bcast(0)
+        w_transpose(0)
+        w_transpose(1)
+        w_quant(0)
+        w_transpose(2)
+        w_quant(1)
+        w_quant(2)
+        g_spread(0)
         for k in (3, 4, 5):
             w_transpose(k)
-        chain_in_b(1)
+        x_factor(1)
         for k in (6, 7, 8):
             w_transpose(k)
-        u_stage(0, [[lambda: w_quant(3), lambda: w_quant(4), lambda: w_quant(5)]])
-        g_bcast(1)
+        u_stage(0, [lambda: w_quant(3), lambda: w_quant(4)], [lambda: w_quant(5)])
+        g_spread(1)
         x_norm(2, 0)
         x_norm(2, 1)
-        chain_in_a(2)
-        u_stage(1, [[]])
-        u_back(0, [lambda: w_quant(6), lambda: w_quant(7), lambda: w_quant(8)])
-        x_chunk(3)
-        g_bcast(2)
+        x_root(2)
+        for k in (6, 7, 8):
+            w_quant(k)
 
-        def tanh_step(s):
+        def closes_alone(s):
+            return s % 4 == 3
+
+        def factor_step(s):
             return s + 3 if s < 4 else s + 2
 
-        def tile_norm(s):
-            out_norm(s, 0)
-            out_norm(s, 1)
-            chain_out_a(s)
-
-        for c in range(NCH + 4):
-            if 1 <= c <= NCH and (c - 1) % 4 < 3:
+        for c in range(N_CHUNKS + 4):
+            if 1 <= c <= N_CHUNKS and not closes_alone(c - 1):
                 for half in range(2):
                     mx_passes(c - 1, half, [2], False, True)
                     relu(c - 1, half)
-            ready = [s for s in range(NCH) if tanh_step(s) == c]
-            if c < NCH:
-                for s in ready:
-                    chain_out_b(s)
-                closes = (c % 4 == 3)
-                mx_passes(c, 0, [0, 1, 2] if closes else [0, 1], True, closes)
-                if closes:
-                    relu(c, 0)
-                if 2 * c + 4 < NCH:
-                    x_chunk(2 * c + 4)
-                mx_passes(c, 1, [0, 1, 2] if closes else [0, 1], True, closes)
-                if closes:
-                    relu(c, 1)
-            fins = [finisher(s, half) for s in range(NCH) if tanh_step(s) + 1 == c for half in range(2)]
-            if c + 2 < NCH:
-                u_stage(c + 2, [fins[0:1]])
-                fins = fins[1:]
-            if c + 1 < NCH:
-                u_back(c + 1, fins)
+            due = [s for s in range(N_CHUNKS) if factor_step(s) == c]
+            if c < N_CHUNKS:
+                for s in due:
+                    tile_factor(s)
+                kernel_rows = [0, 1, 2] if closes_alone(c) else [0, 1]
+                for half in range(2):
+                    mx_passes(c, half, kernel_rows, True, closes_alone(c))
+                    if closes_alone(c):
+                        relu(c, half)
+                    if half == 0 and 2 * c + 3 < N_CHUNKS:
+                        x_chunk(2 * c + 3)
+            finishes = [lambda s=s, half=half: finish(s, half)
+                        for s in range(N_CHUNKS) if factor_step(s) + 1 == c for half in range(2)]
+            if c + 1 < N_CHUNKS:
+                u_stage(c + 1, finishes[0:1], finishes[1:])
             else:
-                for f in fins:
-                    f()
-            if c == 2:
-                chain_in_b(7)
-            if 0 <= c - 1 < NCH:
+                for piece in finishes:
+                    piece()
+            if 2 * c + 3 == N_CHUNKS - 1:
+                x_factor(N_CHUNKS - 1)
+            if 1 <= c <= N_CHUNKS:
                 tile_norm(c - 1)
-            if c >= NCH:
-                for s in ready:
-                    chain_out_b(s)
-            if c + 3 < NCH:
-                g_bcast(c + 3)
-            for s in ready:
-                t_bcast(s)
-            if 2 * c + 5 < NCH:
-                x_chunk(2 * c + 5)
+            if c >= N_CHUNKS:
+                for s in due:
+                    tile_factor(s)
+            if c + 2 < N_CHUNKS:
+                g_spread(c + 2)
+            for s in due:
+                t_spread(s)
+            if 2 * c + 4 < N_CHUNKS:
+                x_chunk(2 * c + 4)

from contextlib import ExitStack

import concourse.mybir as mybir
from concourse.masks import make_identity

FP8X4 = mybir.dt.float8_e4m3fn_x4
BF16 = mybir.dt.bfloat16
F32 = mybir.dt.float32
I32 = mybir.dt.int32
U32 = mybir.dt.uint32
U8 = mybir.dt.uint8
ALU = mybir.AluOpType
ACT = mybir.ActivationFunctionType

P = 128
B, C, O, H, W = 4, 512, 256, 32, 32
FLOPS = 2 * B * H * W * C * 9 * O
Z_MAX = 1.0 - 1e-6
ROWS = 8
PITCH = 64
N_TILE = ROWS * PITCH
N_CHUNKS = 8
PAIR_COLS = (H + 2) * PITCH
N_BLOCKS = 18


def tile_pvconv2d_t_kernel(tc, x, Wk, bias, out):
    nc = tc.nc
    with ExitStack() as ctx:
        ctx.enter_context(tc.manual_schedule())
        const = ctx.enter_context(tc.tile_pool(name="const", bufs=1))
        upool = ctx.enter_context(tc.tile_pool(name="upool", bufs=2))
        junkp = ctx.enter_context(tc.tile_pool(name="junkp", bufs=2))
        rpool = ctx.enter_context(tc.tile_pool(name="rpool", bufs=12))
        opool = ctx.enter_context(tc.tile_pool(name="opool", bufs=6))
        tp = ctx.enter_context(tc.psum_pool(name="tp", bufs=2))
        bc = ctx.enter_context(tc.psum_pool(name="bc", bufs=3))
        accp = ctx.enter_context(tc.psum_pool(name="accp", bufs=3))

        ident_f = const.tile([P, P], F32, name="ident_f")
        make_identity(nc, ident_f[:])
        ident_b = const.tile([P, P], BF16, name="ident_b")
        make_identity(nc, ident_b[:])
        ones1 = const.tile([P, 1], F32, name="ones1")
        nc.vector.memset(ones1[:], 1.0)
        mhalf4 = const.tile([P, 4], F32, name="mhalf4")
        nc.vector.memset(mhalf4[:], -0.5)
        zeros = const.tile([P, 16, 4], BF16, name="zeros")
        nc.vector.memset(zeros[:], 0.0)
        warm = const.tile([P, 1], F32, name="warm")
        nc.scalar.activation(out=warm[:], in_=ones1[:], func=ACT.Ln)
        btile = const.tile([P, P], BF16, name="btile")
        nc.vector.memset(btile[:], 0.0)

        codes = [[const.tile([P, PAIR_COLS], U32, name="codes%d%d" % (j, pair), align_bytes=64) for pair in range(2)]
                 for j in range(3)]
        planes = [[const.tile([P, PAIR_COLS], U8, name="planes%d%d" % (j, pair), align_bytes=64) for pair in range(2)]
                  for j in range(3)]
        u_right = [const.tile([P, 16, 128], BF16, name="ul%d" % k, align_bytes=64) for k in range(2)]
        u_left = [const.tile([P, 16, 128], BF16, name="ur%d" % k, align_bytes=64) for k in range(2)]
        for k in range(2):
            nc.vector.memset(u_right[k][:, :, 0:4], 0.0)
            nc.scalar.copy(out=u_left[k][:, :, 124:128], in_=zeros[:])
        for j in range(3):
            for pair in range(2):
                for lo in (0, PAIR_COLS - PITCH):
                    nc.vector.memset(codes[j][pair][:, lo:lo + PITCH].bitcast(I32), 0)
                    nc.vector.memset(planes[j][pair][:, lo:lo + PITCH].bitcast(I32), 0)

        names = ["n2", "y4", "z2", "zc", "la", "lb", "rzh", "dd", "gg", "m2", "y2o", "zm", "th", "rzo", "tf"]
        sm = dict((nm, const.tile([P, 4 * N_CHUNKS], F32, name="sm_" + nm)) for nm in names)

        def compact(nm, c):
            return sm[nm][:, 4 * c:4 * c + 4]

        xs = [const.tile([P, 4, H * W], BF16, name="xs%d" % b) for b in range(B)]
        w_sb = const.tile([P, N_BLOCKS, C], BF16, name="w_sb")
        wk_v = Wk.rearrange("k (h p) c -> p (k h) c", p=P)

        def load_x_half(b, hh):
            xv = x[b].rearrange("(u q e) h w -> u q e (h w)", u=2, q=P, e=2)
            for u in range(2):
                nc.sync.dma_start(out=xs[b][:, 2 * u:2 * u + 2, hh * 512:(hh + 1) * 512],
                                  in_=xv[u][:, :, hh * 512:(hh + 1) * 512])

        def load_w(kernel_row):
            nc.sync.dma_start(out=w_sb[:, 6 * kernel_row:6 * kernel_row + 6, :],
                              in_=wk_v[:, 6 * kernel_row:6 * kernel_row + 6, :])

        nc.scalar.dma_start(out=btile[0:2, :], in_=bias.rearrange("(h o) -> h o", h=2))
        load_x_half(0, 0)
        load_x_half(1, 0)
        for kernel_row in range(3):
            load_w(kernel_row)
        for b, hh in ((0, 1), (1, 1), (2, 0), (3, 0), (2, 1), (3, 1)):
            load_x_half(b, hh)

        wg = const.tile([P, N_BLOCKS, P, 4], BF16, name="wg", align_bytes=64)
        wc = const.tile([P, N_BLOCKS * P], U32, name="wc", align_bytes=64)
        ws = const.tile([P, N_BLOCKS * P], U8, name="ws", align_bytes=64)
        w_f = w_sb[:].bitcast(F32)
        wg_f = wg[:].bitcast(F32)

        def w_transpose(k):
            wt = accp.tile([P, 2, 2, P], F32, name="wt", tag="acc")
            for bl in range(2):
                for u in range(2):
                    nc.tensor.transpose(wt[:, bl, u, :], w_f[:, 2 * k + bl, u * P:(u + 1) * P], ident_f[:])
            copy = nc.vector.tensor_copy if k < 3 else nc.scalar.copy
            copy(out=wg_f[:, 2 * k:2 * k + 2, :, :], in_=wt[:].rearrange("p b u o -> p b o u"))

        def w_quant(k):
            nc.vector.quantize_mx(
                out=wc[:, 256 * k:256 * k + 256].bitcast(FP8X4),
                scales=ws[:, 256 * k:256 * k + 256],
                in_=wg[:, 2 * k:2 * k + 2, :, :].rearrange("p b o t -> p (b o t)"),
            )

        def x_norm(c, b2):
            pair, hq = divmod(c, 4)
            xf = xs[2 * pair + b2][:].bitcast(F32)
            xt = tp.tile([P, 4, P], F32, name="xt", tag="tp")
            for t in range(4):
                nc.tensor.transpose(xt[:, t, :], xf[:, t, hq * P:(hq + 1) * P], ident_f[:])
            xv = xt[:].bitcast(BF16).rearrange("p t (q par) -> p par t q", par=2)
            for par in range(2):
                junk = junkp.tile([P, 4, P], BF16, name="junk")
                col = 4 * c + 2 * b2 + par
                nc.scalar.activation(out=junk[:], in_=xv[:, par], func=ACT.Square,
                                     accum_out=sm["n2"][:, col:col + 1])

        def x_root(c):
            nc.gpsimd.tensor_scalar(out=compact("y4", c), in0=compact("n2", c), scalar1=0.04, scalar2=4e-16,
                                    op0=ALU.mult, op1=ALU.max)
            nc.gpsimd.tensor_tensor(out=compact("rzh", c), in0=compact("y4", c), in1=mhalf4[:], op=ALU.pow)
            nc.gpsimd.tensor_tensor(out=compact("z2", c), in0=compact("y4", c), in1=compact("rzh", c), op=ALU.mult)
            nc.gpsimd.tensor_scalar(out=compact("zc", c), in0=compact("z2", c), scalar1=0.5, scalar2=Z_MAX,
                                    op0=ALU.mult, op1=ALU.min)

        def x_factor(c):
            nc.scalar.activation(out=compact("la", c), in_=compact("zc", c), func=ACT.Ln, bias=ones1[:], scale=1.0)
            nc.scalar.activation(out=compact("lb", c), in_=compact("zc", c), func=ACT.Ln, bias=ones1[:], scale=-1.0)
            nc.gpsimd.tensor_tensor(out=compact("dd", c), in0=compact("la", c), in1=compact("lb", c), op=ALU.subtract)
            nc.gpsimd.tensor_tensor(out=compact("gg", c), in0=compact("dd", c), in1=compact("rzh", c), op=ALU.mult)

        def x_chunk(c):
            x_norm(c, 0)
            if c > 0:
                x_factor(c - 1)
            x_norm(c, 1)
            x_root(c)

        g_banks = {}

        def g_spread(c):
            gb = bc.tile([P, 4, P], F32, name="gb", tag="bc")
            for k in range(4):
                nc.tensor.transpose(gb[:, k, :], sm["gg"][:, 4 * c + k:4 * c + k + 1].to_broadcast([P, P]), ident_f[:])
            g_banks[c] = gb

        def u_stage(c, fill_a, fill_b):
            pair, hq = divmod(c, 4)
            gb = g_banks[c]
            uc = upool.tile([P, ROWS, 2, W, 4], BF16, name="uc", align_bytes=64)
            for b2 in range(2):
                in0 = xs[2 * pair + b2][:, :, hq * 256:(hq + 1) * 256].rearrange(
                    "p t (h w2 par) -> p h w2 par t", h=ROWS, w2=16, par=2)
                in1 = gb[:, 2 * b2:2 * b2 + 2, :].rearrange("p par (h w2) -> p h w2 par", h=ROWS)
                in1 = in1.unsqueeze(4).to_broadcast([P, ROWS, 16, 2, 4])
                o = uc[:, :, b2, :, :].rearrange("p h (w2 par) t -> p h w2 par t", par=2)
                nc.vector.tensor_tensor(out=o, in0=in0, in1=in1, op=ALU.mult)
            rows = uc[:].rearrange("p h b w t -> p (h b) (w t)")
            k = c % 2
            lo = (ROWS * hq + 1) * PITCH
            sources = [u_right[k][:].rearrange("p r c -> p (r c)"), uc[:].rearrange("p h b w t -> p (h b w t)"),
                       u_left[k][:].rearrange("p r c -> p (r c)")]

            def quant(j):
                nc.vector.quantize_mx(out=codes[j][pair][:, lo:lo + N_TILE].bitcast(FP8X4),
                                      scales=planes[j][pair][:, lo:lo + N_TILE], in_=sources[j])

            nc.scalar.copy(out=u_left[k][:, :, 0:124], in_=rows[:, :, 4:128])
            nc.vector.tensor_copy(out=u_right[k][:, :, 4:128], in_=rows[:, :, 0:124])
            for piece in fill_a:
                piece()
            quant(1)
            quant(0)
            quant(2)
            for piece in fill_b:
                piece()

        accs = {}
        r_tiles = {}

        def mx_passes(s, half, kernel_rows, first, last):
            pair, hq = divmod(s, 4)
            if first:
                acc_new = accp.tile([P, N_TILE], F32, name="acc", tag="acc")
                accs[(s, half)] = acc_new
            acc = accs[(s, half)]
            todo = [(i, j) for j in (1, 0, 2) for i in kernel_rows]
            for n, (i, j) in enumerate(todo):
                blk = 2 * (3 * i + j) + half
                lo = (ROWS * hq + i) * PITCH
                nc.tensor.matmul_mx(
                    out=acc[:],
                    lhsT=wc[:, blk * P:(blk + 1) * P].bitcast(FP8X4),
                    lhsT_scale=ws[:, blk * P:(blk + 1) * P],
                    rhs=codes[j][pair][:, lo:lo + N_TILE].bitcast(FP8X4),
                    rhs_scale=planes[j][pair][:, lo:lo + N_TILE],
                    start=(first and n == 0), stop=(last and n == len(todo) - 1),
                )

        def relu(s, half):
            r = rpool.tile([P, N_TILE], F32, name="r")
            nc.scalar.activation(out=r[:], in_=accs[(s, half)][:], func=ACT.Relu,
                                 bias=bias_sb[:, half:half + 1], scale=1.0)
            r_tiles[(s, half)] = r

        def out_norm(s, pg):
            rt = tp.tile([P, 2, 2, P], F32, name="rt", tag="tp")
            for pl in range(2):
                pb = 2 * pg + pl
                for half in range(2):
                    nc.tensor.transpose(rt[:, pl, half, :], r_tiles[(s, half)][:, pb * P:(pb + 1) * P], ident_f[:])
            for pl in range(2):
                junk = junkp.tile([P, 2, P], BF16, name="junk2")
                col = 4 * s + 2 * pg + pl
                nc.scalar.activation(out=junk[:], in_=rt[:, pl], func=ACT.Square,
                                     accum_out=sm["m2"][:, col:col + 1])

        def tile_norm(s):
            out_norm(s, 0)
            out_norm(s, 1)
            nc.gpsimd.tensor_scalar(out=compact("y2o", s), in0=compact("m2", s), scalar1=0.01, scalar2=1e-16,
                                    op0=ALU.mult, op1=ALU.max)
            nc.gpsimd.tensor_tensor(out=compact("rzo", s), in0=compact("y2o", s), in1=mhalf4[:], op=ALU.pow)
            nc.gpsimd.tensor_tensor(out=compact("zm", s), in0=compact("y2o", s), in1=compact("rzo", s), op=ALU.mult)

        def tile_factor(s):
            nc.scalar.activation(out=compact("th", s), in_=compact("zm", s), func=ACT.Tanh)
            nc.gpsimd.tensor_tensor(out=compact("tf", s), in0=compact("th", s), in1=compact("rzo", s), op=ALU.mult)

        t_banks = {}

        def t_spread(s):
            tb = bc.tile([P, 4, P], F32, name="tb", tag="bc")
            for k in range(4):
                nc.tensor.transpose(tb[:, k, :], sm["tf"][:, 4 * s + k:4 * s + k + 1].to_broadcast([P, P]), ident_f[:])
            t_banks[s] = tb

        def finish(s, half):
            pair, hq = divmod(s, 4)
            tv = t_banks[s][:].rearrange("p k (a b w) -> p (k a) b w", a=2, b=2)
            ob = opool.tile([P, 2, ROWS, W], F32, name="ob")
            rv = r_tiles[(s, half)][:].rearrange("p (h b w) -> p h b w", h=ROWS, b=2)
            nc.vector.tensor_tensor(out=ob[:].rearrange("p b h w -> p h b w"), in0=rv, in1=tv, op=ALU.mult)
            nc.sync.dma_start(
                out=out[2 * pair:2 * pair + 2, half * P:(half + 1) * P, ROWS * hq:ROWS * hq + ROWS, :].rearrange(
                    "b p h w -> p b (h w)"),
                in_=ob[:].rearrange("p b h w -> p b (h w)"),
            )

        bt = tp.tile([P, P], BF16, name="bt", tag="tp")
        nc.tensor.transpose(bt[:], btile[:], ident_b[:])
        bias_sb = const.tile([P, 2], F32, name="bias_sb")
        nc.vector.tensor_copy(out=bias_sb[:], in_=bt[:, 0:2])
        x_chunk(0)
        x_chunk(1)
        w_transpose(0)
        w_transpose(1)
        w_quant(0)
        w_transpose(2)
        w_quant(1)
        w_quant(2)
        g_spread(0)
        for k in (3, 4, 5):
            w_transpose(k)
        x_factor(1)
        for k in (6, 7, 8):
            w_transpose(k)
        u_stage(0, [lambda: w_quant(3), lambda: w_quant(4)], [lambda: w_quant(5)])
        g_spread(1)
        x_norm(2, 0)
        x_norm(2, 1)
        x_root(2)
        for k in (6, 7, 8):
            w_quant(k)

        def closes_alone(s):
            return s % 4 == 3

        def factor_step(s):
            return s + 3 if s < 4 else s + 2

        for c in range(N_CHUNKS + 4):
            if 1 <= c <= N_CHUNKS and not closes_alone(c - 1):
                for half in range(2):
                    mx_passes(c - 1, half, [2], False, True)
                    relu(c - 1, half)
            due = [s for s in range(N_CHUNKS) if factor_step(s) == c]
            if c < N_CHUNKS:
                for s in due:
                    tile_factor(s)
                kernel_rows = [0, 1, 2] if closes_alone(c) else [0, 1]
                for half in range(2):
                    mx_passes(c, half, kernel_rows, True, closes_alone(c))
                    if closes_alone(c):
                        relu(c, half)
                    if half == 0 and 2 * c + 3 < N_CHUNKS:
                        x_chunk(2 * c + 3)
            finishes = [lambda s=s, half=half: finish(s, half)
                        for s in range(N_CHUNKS) if factor_step(s) + 1 == c for half in range(2)]
            if c + 1 < N_CHUNKS:
                u_stage(c + 1, finishes[0:1], finishes[1:])
            else:
                for piece in finishes:
                    piece()
            if 2 * c + 3 == N_CHUNKS - 1:
                x_factor(N_CHUNKS - 1)
            if 1 <= c <= N_CHUNKS:
                tile_norm(c - 1)
            if c >= N_CHUNKS:
                for s in due:
                    tile_factor(s)
            if c + 2 < N_CHUNKS:
                g_spread(c + 2)
            for s in due:
                t_spread(s)
            if 2 * c + 4 < N_CHUNKS:
                x_chunk(2 * c + 4)
